import numpy as np
import ml_dtypes


def mxq(x, axis, fmt="e4m3"):
    dtype, down = {"e4m3": (ml_dtypes.float8_e4m3fn, 7), "e5m2": (ml_dtypes.float8_e5m2, 14)}[fmt]
    v = np.moveaxis(np.asarray(x, np.float32).astype(ml_dtypes.bfloat16).astype(np.float64), axis, -1)
    blocks = v.reshape(v.shape[:-1] + (-1, 32))
    amax = np.abs(blocks).max(-1, keepdims=True)
    byte = np.maximum(np.where(amax > 0, np.frexp(amax)[1] - 1 + 127, 0) - down, 1)
    scale = np.exp2(byte - 127.0)
    codes = (blocks / scale).astype(np.float32).astype(dtype).astype(np.float64)
    return np.moveaxis((codes * scale).reshape(v.shape), -1, axis)


WIDE = False


def mx_kscale(k):
    if not WIDE:
        return np.ones(k)
    levels = np.array([10, -10, 5, -5, 0])
    a = np.random.permutation(np.resize(levels, k // 512 * 4)).reshape(k // 512, 4)
    idx = np.arange(k)
    return np.exp2(a[idx // 512, idx % 128 // 32])


BF16 = ml_dtypes.bfloat16


def bf(x):
    return np.asarray(x, np.float32).astype(BF16)


def f64(x):
    return np.asarray(x).astype(np.float64)


B, X_DIM, Z_DIM, K, H = 256, 1024, 64, 512, 512


def elu(v):
    return np.where(v > 0.0, v, np.exp(np.minimum(v, 0.0)) - 1.0)


def softplus(v):
    return np.maximum(v, 0.0) + np.log(1.0 + np.exp(-np.abs(v)))


def setup_inputs():
    s = mx_kscale(H)
    return {"dec_h1": bf(elu(np.random.standard_normal((B, H))) * s),
            "x": bf(np.random.random((B, X_DIM))),
            "dw2": bf(np.random.standard_normal((H, H)) * 1.25 / np.sqrt(H) / s[:, None]),
            "db2": bf(np.random.standard_normal(H) * 0.5),
            "dw3": bf(np.random.standard_normal((H, X_DIM)) * 2.5 / np.sqrt(H)),
            "db3": bf(np.random.standard_normal(X_DIM) * 0.8)}


def reference(dec_h1, x, dw2, db2, dw3, db3):
    d2 = elu((mxq(f64(dec_h1), 1, "e4m3") @ mxq(f64(dw2), 0, "e4m3")) + f64(db2))
    logits = (mxq(d2, 1, "e4m3") @ mxq(f64(dw3), 0, "e4m3")) + f64(db3)
    return np.sum(f64(x) * logits - softplus(logits), axis=-1)

@@ -1,0 +1,248 @@
+from contextlib import ExitStack
+
+import concourse.mybir as mybir
+from concourse.masks import make_identity
+
+F32 = mybir.dt.float32
+BF16 = mybir.dt.bfloat16
+U32 = mybir.dt.uint32
+U8 = mybir.dt.uint8
+FP8X4 = mybir.dt.float8_e4m3fn_x4
+ALU = mybir.AluOpType
+ACT = mybir.ActivationFunctionType
+AXIS = mybir.AxisListType
+
+P = 128
+PACK = 4
+BATCH = 256
+HIDDEN = 512
+PIXELS = 1024
+B_TILES = BATCH // P
+BANK = 512
+J_HALVES = PIXELS // BANK
+RUN = 4
+FACTORS = 32
+
+FLOPS = 2 * BATCH * HIDDEN * HIDDEN + 2 * BATCH * HIDDEN * PIXELS
+
+
+def regroup(copy, grouped, rows):
+    copy(
+        out=grouped.rearrange("p (c i) t -> p c t i", i=RUN),
+        in_=rows.rearrange("p t (c i) -> p c t i", i=RUN),
+    )
+
+
+def quantise(nc, grouped, codes, scales):
+    nc.vector.quantize_mx(
+        out=codes.bitcast(FP8X4),
+        scales=scales,
+        in_=grouped.rearrange("p w t -> p (w t)"),
+    )
+
+
+def tile_gmvae_pb_s_kernel(tc, dec_h1, x, dw2, db2, dw3, db3, out):
+    nc = tc.nc
+    with ExitStack() as ctx:
+        keep = ctx.enter_context(tc.tile_pool(name="keep", bufs=1))
+        psum = ctx.enter_context(tc.psum_pool(name="psum", bufs=8))
+
+        ctx.enter_context(tc.manual_schedule())
+
+        b2_rows = keep.tile([P, P], BF16)
+        nc.gpsimd.memset(b2_rows[:], 0.0)
+        b3_row = keep.tile([P, PIXELS], BF16)
+        nc.vector.memset(b3_row[:], 0.0)
+        ones = keep.tile([P, P], BF16)
+        nc.vector.memset(ones[:], 1.0)
+        warm = keep.tile([P, 1], F32)
+        nc.vector.memset(warm[:], 0.0)
+        res_pad = keep.tile([P, P], F32)
+        nc.vector.memset(res_pad[:], 0.0)
+        ident_f32 = keep.tile([P, P], F32)
+        make_identity(nc, ident_f32[:])
+        ident_bf16 = keep.tile([P, P], BF16)
+        make_identity(nc, ident_bf16[:])
+        nc.scalar.activation(out=warm[:], in_=warm[:], func=ACT.Exp)
+
+        nc.sync.dma_start(out=b2_rows[0:PACK, :], in_=db2.rearrange("(t p) -> t p", p=P))
+        a_rows = keep.tile([P, B_TILES, HIDDEN], BF16)
+        nc.sync.dma_start(out=a_rows[:], in_=dec_h1.rearrange("(i p) k -> p i k", p=P))
+        nc.sync.dma_start(out=b3_row[0:1, :], in_=db3.rearrange("(o j) -> o j", o=1))
+        w2_rows = keep.tile([P, PACK, HIDDEN], BF16)
+        nc.sync.dma_start(
+            out=w2_rows[:].rearrange("p (u e) h -> p u e h", u=2),
+            in_=dw2.rearrange("(u p e) h -> p u e h", u=2, e=2),
+        )
+        w3_rows = []
+        for jh in range(J_HALVES):
+            rows = keep.tile([P, PACK, BANK], BF16, name="w3_rows%d" % jh)
+            nc.sync.dma_start(
+                out=rows[:],
+                in_=dw3[:, jh * BANK : (jh + 1) * BANK].rearrange("(t p) j -> p t j", p=P),
+            )
+            w3_rows.append(rows)
+        x_rows = keep.tile([P, B_TILES, PIXELS], BF16)
+        nc.sync.dma_start(out=x_rows[:], in_=x.rearrange("(i p) j -> p i j", p=P))
+
+        a_words = a_rows[:].bitcast(F32)
+        aT_bank = psum.tile([P, 2, BATCH], F32, tag="bank")
+        for u in range(2):
+            for i in range(B_TILES):
+                nc.tensor.transpose(
+                    aT_bank[:, u, i * P : (i + 1) * P], a_words[:, i, u * P : (u + 1) * P], ident_f32[:]
+                )
+        a_grouped = keep.tile([P, BATCH, PACK], BF16, align_bytes=64)
+        nc.scalar.copy(out=a_grouped[:].bitcast(F32), in_=aT_bank[:].rearrange("p u b -> p b u"))
+
+        b2_bank = psum.tile([P, P], BF16, tag="bank")
+        nc.tensor.transpose(b2_bank[:], b2_rows[:], ident_bf16[:])
+        b2 = keep.tile([P, PACK], F32)
+        nc.vector.tensor_copy(out=b2[:], in_=b2_bank[:, 0:PACK])
+        b3_all = keep.tile([P, PIXELS], F32)
+        for jh in range(J_HALVES):
+            cols = slice(jh * BANK, (jh + 1) * BANK)
+            b3_bank = psum.tile([P, BANK], F32, tag="bank")
+            nc.tensor.matmul(out=b3_bank[:], lhsT=ones[:], rhs=b3_row[:, cols], start=True, stop=True)
+            nc.scalar.copy(out=b3_all[:, cols], in_=b3_bank[:])
+
+        w2_grouped = keep.tile([P, HIDDEN, PACK], BF16, align_bytes=64)
+        regroup(nc.vector.tensor_copy, w2_grouped[:], w2_rows[:])
+        a_codes = keep.tile([P, BATCH], U32, align_bytes=64)
+        a_scales = keep.tile([P, BATCH], U8, align_bytes=64)
+        quantise(nc, a_grouped[:], a_codes[:], a_scales[:])
+        w2_codes = keep.tile([P, HIDDEN], U32, align_bytes=64)
+        w2_scales = keep.tile([P, HIDDEN], U8, align_bytes=64)
+        quantise(nc, w2_grouped[:], w2_codes[:], w2_scales[:])
+
+        z_banks = []
+        for half in range(2):
+            z_bank = psum.tile([P, 2, BATCH], F32, tag="bank")
+            for s in range(2):
+                h_cols = slice((2 * half + s) * P, (2 * half + s + 1) * P)
+                nc.tensor.matmul_mx(
+                    out=z_bank[:, s, :],
+                    lhsT=w2_codes[:, h_cols].bitcast(FP8X4),
+                    lhsT_scale=w2_scales[:, h_cols],
+                    rhs=a_codes[:].bitcast(FP8X4),
+                    rhs_scale=a_scales[:],
+                    start=True,
+                    stop=True,
+                )
+            z_banks.append(z_bank)
+
+        w3_grouped = []
+        for jh in range(J_HALVES):
+            grouped = keep.tile([P, BANK, PACK], BF16, align_bytes=64, name="w3_grouped%d" % jh)
+            w3_grouped.append(grouped)
+        w3_codes = keep.tile([P, J_HALVES, BANK], U32, align_bytes=64)
+        w3_scales = keep.tile([P, J_HALVES, BANK], U8, align_bytes=64)
+        regroup(nc.vector.tensor_copy, w3_grouped[0][:], w3_rows[0][:])
+
+        neg = keep.tile([P, PACK, BATCH], F32)
+        d2_rows = keep.tile([P, PACK, BATCH], BF16)
+        for half in range(2):
+            pair = slice(2 * half, 2 * half + 2)
+            for s in range(2):
+                t = 2 * half + s
+                nc.scalar.activation(
+                    out=neg[:, t, :], in_=z_banks[half][:, s, :], func=ACT.Exp, bias=b2[:, t : t + 1], scale=1.0
+                )
+            nc.vector.tensor_scalar(
+                out=neg[:, pair, :], in0=neg[:, pair, :], scalar1=-1.0, scalar2=0.0, op0=ALU.add, op1=ALU.min
+            )
+            for s in range(2):
+                t = 2 * half + s
+                nc.vector.scalar_tensor_tensor(
+                    out=d2_rows[:, t, :],
+                    in0=z_banks[half][:, s, :],
+                    scalar=b2[:, t : t + 1],
+                    in1=neg[:, t, :],
+                    op0=ALU.add,
+                    op1=ALU.max,
+                )
+        regroup(nc.scalar.copy, w3_grouped[1][:], w3_rows[1][:])
+        nc.scalar.activation(out=warm[:], in_=warm[:], func=ACT.Sigmoid)
+        d2_grouped = keep.tile([P, BATCH, PACK], BF16, align_bytes=64)
+        regroup(nc.vector.tensor_copy, d2_grouped[:], d2_rows[:])
+        quantise(nc, w3_grouped[0][:], w3_codes[:, 0, :], w3_scales[:, 0, :])
+        d2_codes = keep.tile([P, BATCH], U32, align_bytes=64)
+        d2_scales = keep.tile([P, BATCH], U8, align_bytes=64)
+        quantise(nc, d2_grouped[:], d2_codes[:], d2_scales[:])
+        quantise(nc, w3_grouped[1][:], w3_codes[:, 1, :], w3_scales[:, 1, :])
+
+        acc_xv = keep.tile([P, B_TILES, J_HALVES], F32)
+        acc_abs = keep.tile([P, B_TILES, J_HALVES], F32)
+        acc_ln = keep.tile([P, B_TILES], F32)
+        products = keep.tile([P, B_TILES, J_HALVES, BANK // FACTORS], F32)
+        banks = [(jh, i) for jh in range(J_HALVES) for i in range(B_TILES)]
+        v_all = keep.tile([P, len(banks), BANK], F32)
+        sig = keep.tile([P, len(banks), BANK], F32)
+        junk = keep.tile([P, len(banks), BANK], F32)
+
+        def weighted_sum(n):
+            jh, i = banks[n]
+            nc.vector.scalar_tensor_tensor(
+                out=junk[:, n, :],
+                in0=x_rows[:, i, jh * BANK : (jh + 1) * BANK],
+                scalar=-0.5,
+                in1=v_all[:, n, :],
+                op0=ALU.add,
+                op1=ALU.mult,
+                accum_out=acc_xv[:, i, jh : jh + 1],
+            )
+
+        def multiply_up(n):
+            jh, i = banks[n]
+            nc.vector.tensor_reduce(
+                out=products[:, i, jh, :],
+                in_=sig[:, n, :].rearrange("p (g f) -> p g f", f=FACTORS),
+                axis=AXIS.X,
+                op=ALU.mult,
+            )
+
+        for n, (jh, i) in enumerate(banks):
+            b_cols = slice(i * P, (i + 1) * P)
+            logit_bank = psum.tile([P, BANK], F32, tag="bank")
+            nc.tensor.matmul_mx(
+                out=logit_bank[:],
+                lhsT=d2_codes[:, b_cols].bitcast(FP8X4),
+                lhsT_scale=d2_scales[:, b_cols],
+                rhs=w3_codes[:, jh, :].bitcast(FP8X4),
+                rhs_scale=w3_scales[:, jh, :],
+                start=True,
+                stop=True,
+            )
+            nc.vector.tensor_tensor(
+                out=v_all[:, n, :], in0=logit_bank[:], in1=b3_all[:, jh * BANK : (jh + 1) * BANK], op=ALU.add
+            )
+            nc.scalar.activation(
+                out=sig[:, n, :], in_=v_all[:, n, :], func=ACT.Abs, scale=0.5, accum_out=acc_abs[:, i, jh : jh + 1]
+            )
+            nc.scalar.activation(out=sig[:, n, :], in_=sig[:, n, :], func=ACT.Sigmoid, scale=2.0)
+        nc.scalar.activation(out=warm[:], in_=warm[:], func=ACT.Ln)
+        weighted_sum(0)
+        weighted_sum(1)
+        for n in range(len(banks)):
+            multiply_up(n)
+        weighted_sum(2)
+        weighted_sum(3)
+        ln_products = keep.tile([P, B_TILES, J_HALVES * (BANK // FACTORS)], F32)
+        for i in range(B_TILES):
+            nc.scalar.activation(
+                out=ln_products[:, i, :],
+                in_=products[:, i, :, :].rearrange("p j g -> p (j g)"),
+                func=ACT.Ln,
+                accum_out=acc_ln[:, i : i + 1],
+            )
+
+        partial = keep.tile([P, B_TILES, J_HALVES], F32)
+        nc.vector.tensor_tensor(out=partial[:], in0=acc_xv[:], in1=acc_abs[:], op=ALU.subtract)
+        summed = keep.tile([P, B_TILES], F32)
+        nc.vector.tensor_reduce(out=summed[:], in_=partial[:], axis=AXIS.X, op=ALU.add)
+        nc.vector.tensor_tensor(out=res_pad[:, 0:B_TILES], in0=summed[:], in1=acc_ln[:], op=ALU.add)
+        resT_bank = psum.tile([P, P], F32, tag="bank")
+        nc.tensor.transpose(resT_bank[:], res_pad[:], ident_f32[:])
+        res_rows = keep.tile([B_TILES, P], F32)
+        nc.vector.tensor_copy(out=res_rows[:], in_=resT_bank[0:B_TILES, :])
+        nc.sync.dma_start(out=out.rearrange("(i p) -> i p", p=P), in_=res_rows[:])

@@ -50,7 +50,7 @@ def tile_gmvae_pb_s_kernel(tc, dec_h1, x, dw2, db2, dw3, db3, out):
         ctx.enter_context(tc.manual_schedule())
 
         b2_rows = keep.tile([P, P], BF16)
-        nc.gpsimd.memset(b2_rows[:], 0.0)
+        nc.vector.memset(b2_rows[:], 0.0)
         b3_row = keep.tile([P, PIXELS], BF16)
         nc.vector.memset(b3_row[:], 0.0)
         ones = keep.tile([P, P], BF16)
@@ -63,12 +63,12 @@ def tile_gmvae_pb_s_kernel(tc, dec_h1, x, dw2, db2, dw3, db3, out):
         make_identity(nc, ident_f32[:])
         ident_bf16 = keep.tile([P, P], BF16)
         make_identity(nc, ident_bf16[:])
-        nc.scalar.activation(out=warm[:], in_=warm[:], func=ACT.Exp)
 
-        nc.sync.dma_start(out=b2_rows[0:PACK, :], in_=db2.rearrange("(t p) -> t p", p=P))
+        nc.scalar.dma_start(out=b2_rows[0:PACK, :], in_=db2.rearrange("(t p) -> t p", p=P))
+        nc.scalar.dma_start(out=b3_row[0:1, :], in_=db3.rearrange("(o j) -> o j", o=1))
+        nc.scalar.activation(out=warm[:], in_=warm[:], func=ACT.Exp)
         a_rows = keep.tile([P, B_TILES, HIDDEN], BF16)
         nc.sync.dma_start(out=a_rows[:], in_=dec_h1.rearrange("(i p) k -> p i k", p=P))
-        nc.sync.dma_start(out=b3_row[0:1, :], in_=db3.rearrange("(o j) -> o j", o=1))
         w2_rows = keep.tile([P, PACK, HIDDEN], BF16)
         nc.sync.dma_start(
             out=w2_rows[:].rearrange("p (u e) h -> p u e h", u=2),
@@ -98,7 +98,7 @@ def tile_gmvae_pb_s_kernel(tc, dec_h1, x, dw2, db2, dw3, db3, out):
         b2_bank = psum.tile([P, P], BF16, tag="bank")
         nc.tensor.transpose(b2_bank[:], b2_rows[:], ident_bf16[:])
         b2 = keep.tile([P, PACK], F32)
-        nc.vector.tensor_copy(out=b2[:], in_=b2_bank[:, 0:PACK])
+        nc.scalar.copy(out=b2[:], in_=b2_bank[:, 0:PACK])
         b3_all = keep.tile([P, PIXELS], F32)
         for jh in range(J_HALVES):
             cols = slice(jh * BANK, (jh + 1) * BANK)
@@ -107,13 +107,16 @@ def tile_gmvae_pb_s_kernel(tc, dec_h1, x, dw2, db2, dw3, db3, out):
             nc.scalar.copy(out=b3_all[:, cols], in_=b3_bank[:])
 
         w2_grouped = keep.tile([P, HIDDEN, PACK], BF16, align_bytes=64)
-        regroup(nc.vector.tensor_copy, w2_grouped[:], w2_rows[:])
+        w2_halves = [slice(0, HIDDEN // 2), slice(HIDDEN // 2, HIDDEN)]
+        for h_half in w2_halves:
+            regroup(nc.vector.tensor_copy, w2_grouped[:, h_half, :], w2_rows[:, :, h_half])
         a_codes = keep.tile([P, BATCH], U32, align_bytes=64)
         a_scales = keep.tile([P, BATCH], U8, align_bytes=64)
         quantise(nc, a_grouped[:], a_codes[:], a_scales[:])
         w2_codes = keep.tile([P, HIDDEN], U32, align_bytes=64)
         w2_scales = keep.tile([P, HIDDEN], U8, align_bytes=64)
-        quantise(nc, w2_grouped[:], w2_codes[:], w2_scales[:])
+        for h_half in w2_halves:
+            quantise(nc, w2_grouped[:, h_half, :], w2_codes[:, h_half], w2_scales[:, h_half])
 
         z_banks = []
         for half in range(2):
@@ -164,11 +167,14 @@ def tile_gmvae_pb_s_kernel(tc, dec_h1, x, dw2, db2, dw3, db3, out):
         regroup(nc.scalar.copy, w3_grouped[1][:], w3_rows[1][:])
         nc.scalar.activation(out=warm[:], in_=warm[:], func=ACT.Sigmoid)
         d2_grouped = keep.tile([P, BATCH, PACK], BF16, align_bytes=64)
-        regroup(nc.vector.tensor_copy, d2_grouped[:], d2_rows[:])
+        b_tiles = [slice(i * P, (i + 1) * P) for i in range(B_TILES)]
+        for b_cols in b_tiles:
+            regroup(nc.vector.tensor_copy, d2_grouped[:, b_cols, :], d2_rows[:, :, b_cols])
         quantise(nc, w3_grouped[0][:], w3_codes[:, 0, :], w3_scales[:, 0, :])
         d2_codes = keep.tile([P, BATCH], U32, align_bytes=64)
         d2_scales = keep.tile([P, BATCH], U8, align_bytes=64)
-        quantise(nc, d2_grouped[:], d2_codes[:], d2_scales[:])
+        for b_cols in b_tiles:
+            quantise(nc, d2_grouped[:, b_cols, :], d2_codes[:, b_cols], d2_scales[:, b_cols])
         quantise(nc, w3_grouped[1][:], w3_codes[:, 1, :], w3_scales[:, 1, :])
 
         acc_xv = keep.tile([P, B_TILES, J_HALVES], F32)
@@ -202,7 +208,7 @@ def tile_gmvae_pb_s_kernel(tc, dec_h1, x, dw2, db2, dw3, db3, out):
             )
 
         for n, (jh, i) in enumerate(banks):
-            b_cols = slice(i * P, (i + 1) * P)
+            b_cols = b_tiles[i]
             logit_bank = psum.tile([P, BANK], F32, tag="bank")
             nc.tensor.matmul_mx(
                 out=logit_bank[:],

@@ -50,11 +50,7 @@ def tile_gmvae_pb_s_kernel(tc, dec_h1, x, dw2, db2, dw3, db3, out):
         ctx.enter_context(tc.manual_schedule())
 
         b2_rows = keep.tile([P, P], BF16)
-        nc.vector.memset(b2_rows[:], 0.0)
-        b3_row = keep.tile([P, PIXELS], BF16)
-        nc.vector.memset(b3_row[:], 0.0)
-        ones = keep.tile([P, P], BF16)
-        nc.vector.memset(ones[:], 1.0)
+        nc.gpsimd.memset(b2_rows[:], 0.0)
         warm = keep.tile([P, 1], F32)
         nc.vector.memset(warm[:], 0.0)
         res_pad = keep.tile([P, P], F32)
@@ -63,12 +59,11 @@ def tile_gmvae_pb_s_kernel(tc, dec_h1, x, dw2, db2, dw3, db3, out):
         make_identity(nc, ident_f32[:])
         ident_bf16 = keep.tile([P, P], BF16)
         make_identity(nc, ident_bf16[:])
-
-        nc.scalar.dma_start(out=b2_rows[0:PACK, :], in_=db2.rearrange("(t p) -> t p", p=P))
-        nc.scalar.dma_start(out=b3_row[0:1, :], in_=db3.rearrange("(o j) -> o j", o=1))
         nc.scalar.activation(out=warm[:], in_=warm[:], func=ACT.Exp)
+
         a_rows = keep.tile([P, B_TILES, HIDDEN], BF16)
         nc.sync.dma_start(out=a_rows[:], in_=dec_h1.rearrange("(i p) k -> p i k", p=P))
+        nc.sync.dma_start(out=b2_rows[0:PACK, :], in_=db2.rearrange("(t p) -> t p", p=P))
         w2_rows = keep.tile([P, PACK, HIDDEN], BF16)
         nc.sync.dma_start(
             out=w2_rows[:].rearrange("p (u e) h -> p u e h", u=2),
@@ -82,6 +77,8 @@ def tile_gmvae_pb_s_kernel(tc, dec_h1, x, dw2, db2, dw3, db3, out):
                 in_=dw3[:, jh * BANK : (jh + 1) * BANK].rearrange("(t p) j -> p t j", p=P),
             )
             w3_rows.append(rows)
+        b3_all = keep.tile([P, PIXELS], BF16)
+        nc.sync.dma_start(out=b3_all[:], in_=db3.partition_broadcast(P))
         x_rows = keep.tile([P, B_TILES, PIXELS], BF16)
         nc.sync.dma_start(out=x_rows[:], in_=x.rearrange("(i p) j -> p i j", p=P))
 
@@ -95,21 +92,15 @@ def tile_gmvae_pb_s_kernel(tc, dec_h1, x, dw2, db2, dw3, db3, out):
         a_grouped = keep.tile([P, BATCH, PACK], BF16, align_bytes=64)
         nc.scalar.copy(out=a_grouped[:].bitcast(F32), in_=aT_bank[:].rearrange("p u b -> p b u"))
 
+
+        w2_grouped = keep.tile([P, HIDDEN, PACK], BF16, align_bytes=64)
+        w2_halves = [slice(0, HIDDEN // 2), slice(HIDDEN // 2, HIDDEN)]
+        regroup(nc.vector.tensor_copy, w2_grouped[:, w2_halves[0], :], w2_rows[:, :, w2_halves[0]])
+        regroup(nc.scalar.copy, w2_grouped[:, w2_halves[1], :], w2_rows[:, :, w2_halves[1]])
         b2_bank = psum.tile([P, P], BF16, tag="bank")
         nc.tensor.transpose(b2_bank[:], b2_rows[:], ident_bf16[:])
         b2 = keep.tile([P, PACK], F32)
         nc.scalar.copy(out=b2[:], in_=b2_bank[:, 0:PACK])
-        b3_all = keep.tile([P, PIXELS], F32)
-        for jh in range(J_HALVES):
-            cols = slice(jh * BANK, (jh + 1) * BANK)
-            b3_bank = psum.tile([P, BANK], F32, tag="bank")
-            nc.tensor.matmul(out=b3_bank[:], lhsT=ones[:], rhs=b3_row[:, cols], start=True, stop=True)
-            nc.scalar.copy(out=b3_all[:, cols], in_=b3_bank[:])
-
-        w2_grouped = keep.tile([P, HIDDEN, PACK], BF16, align_bytes=64)
-        w2_halves = [slice(0, HIDDEN // 2), slice(HIDDEN // 2, HIDDEN)]
-        for h_half in w2_halves:
-            regroup(nc.vector.tensor_copy, w2_grouped[:, h_half, :], w2_rows[:, :, h_half])
         a_codes = keep.tile([P, BATCH], U32, align_bytes=64)
         a_scales = keep.tile([P, BATCH], U8, align_bytes=64)
         quantise(nc, a_grouped[:], a_codes[:], a_scales[:])
@@ -177,76 +168,56 @@ def tile_gmvae_pb_s_kernel(tc, dec_h1, x, dw2, db2, dw3, db3, out):
             quantise(nc, d2_grouped[:, b_cols, :], d2_codes[:, b_cols], d2_scales[:, b_cols])
         quantise(nc, w3_grouped[1][:], w3_codes[:, 1, :], w3_scales[:, 1, :])
 
-        acc_xv = keep.tile([P, B_TILES, J_HALVES], F32)
+        v_all = keep.tile([P, B_TILES, PIXELS], F32)
+        sig = keep.tile([P, B_TILES, PIXELS], F32)
         acc_abs = keep.tile([P, B_TILES, J_HALVES], F32)
-        acc_ln = keep.tile([P, B_TILES], F32)
-        products = keep.tile([P, B_TILES, J_HALVES, BANK // FACTORS], F32)
-        banks = [(jh, i) for jh in range(J_HALVES) for i in range(B_TILES)]
-        v_all = keep.tile([P, len(banks), BANK], F32)
-        sig = keep.tile([P, len(banks), BANK], F32)
-        junk = keep.tile([P, len(banks), BANK], F32)
+        for jh in range(J_HALVES):
+            cols = slice(jh * BANK, (jh + 1) * BANK)
+            for i in range(B_TILES):
+                logit_bank = psum.tile([P, BANK], F32, tag="bank")
+                nc.tensor.matmul_mx(
+                    out=logit_bank[:],
+                    lhsT=d2_codes[:, b_tiles[i]].bitcast(FP8X4),
+                    lhsT_scale=d2_scales[:, b_tiles[i]],
+                    rhs=w3_codes[:, jh, :].bitcast(FP8X4),
+                    rhs_scale=w3_scales[:, jh, :],
+                    start=True,
+                    stop=True,
+                )
+                nc.vector.tensor_tensor(out=v_all[:, i, cols], in0=logit_bank[:], in1=b3_all[:, cols], op=ALU.add)
+                nc.scalar.activation(
+                    out=sig[:, i, cols], in_=v_all[:, i, cols], func=ACT.Abs, scale=0.5, accum_out=acc_abs[:, i, jh : jh + 1]
+                )
+                nc.scalar.activation(out=sig[:, i, cols], in_=sig[:, i, cols], func=ACT.Sigmoid, scale=2.0)
+        nc.scalar.activation(out=warm[:], in_=warm[:], func=ACT.Ln)
 
-        def weighted_sum(n):
-            jh, i = banks[n]
+        acc_xv = keep.tile([P, B_TILES], F32)
+        junk = keep.tile([P, PIXELS], F32)
+        for i in range(B_TILES):
             nc.vector.scalar_tensor_tensor(
-                out=junk[:, n, :],
-                in0=x_rows[:, i, jh * BANK : (jh + 1) * BANK],
+                out=junk[:],
+                in0=x_rows[:, i, :],
                 scalar=-0.5,
-                in1=v_all[:, n, :],
+                in1=v_all[:, i, :],
                 op0=ALU.add,
                 op1=ALU.mult,
-                accum_out=acc_xv[:, i, jh : jh + 1],
+                accum_out=acc_xv[:, i : i + 1],
             )
-
-        def multiply_up(n):
-            jh, i = banks[n]
+        products = keep.tile([P, B_TILES, PIXELS // FACTORS], F32)
+        acc_ln = keep.tile([P, B_TILES], F32)
+        for i in range(B_TILES):
             nc.vector.tensor_reduce(
-                out=products[:, i, jh, :],
-                in_=sig[:, n, :].rearrange("p (g f) -> p g f", f=FACTORS),
+                out=products[:, i, :],
+                in_=sig[:, i, :].rearrange("p (g f) -> p g f", f=FACTORS),
                 axis=AXIS.X,
                 op=ALU.mult,
             )
+            nc.scalar.activation(out=products[:, i, :], in_=products[:, i, :], func=ACT.Ln, accum_out=acc_ln[:, i : i + 1])
 
-        for n, (jh, i) in enumerate(banks):
-            b_cols = b_tiles[i]
-            logit_bank = psum.tile([P, BANK], F32, tag="bank")
-            nc.tensor.matmul_mx(
-                out=logit_bank[:],
-                lhsT=d2_codes[:, b_cols].bitcast(FP8X4),
-                lhsT_scale=d2_scales[:, b_cols],
-                rhs=w3_codes[:, jh, :].bitcast(FP8X4),
-                rhs_scale=w3_scales[:, jh, :],
-                start=True,
-                stop=True,
-            )
-            nc.vector.tensor_tensor(
-                out=v_all[:, n, :], in0=logit_bank[:], in1=b3_all[:, jh * BANK : (jh + 1) * BANK], op=ALU.add
-            )
-            nc.scalar.activation(
-                out=sig[:, n, :], in_=v_all[:, n, :], func=ACT.Abs, scale=0.5, accum_out=acc_abs[:, i, jh : jh + 1]
-            )
-            nc.scalar.activation(out=sig[:, n, :], in_=sig[:, n, :], func=ACT.Sigmoid, scale=2.0)
-        nc.scalar.activation(out=warm[:], in_=warm[:], func=ACT.Ln)
-        weighted_sum(0)
-        weighted_sum(1)
-        for n in range(len(banks)):
-            multiply_up(n)
-        weighted_sum(2)
-        weighted_sum(3)
-        ln_products = keep.tile([P, B_TILES, J_HALVES * (BANK // FACTORS)], F32)
-        for i in range(B_TILES):
-            nc.scalar.activation(
-                out=ln_products[:, i, :],
-                in_=products[:, i, :, :].rearrange("p j g -> p (j g)"),
-                func=ACT.Ln,
-                accum_out=acc_ln[:, i : i + 1],
-            )
-
-        partial = keep.tile([P, B_TILES, J_HALVES], F32)
-        nc.vector.tensor_tensor(out=partial[:], in0=acc_xv[:], in1=acc_abs[:], op=ALU.subtract)
-        summed = keep.tile([P, B_TILES], F32)
-        nc.vector.tensor_reduce(out=summed[:], in_=partial[:], axis=AXIS.X, op=ALU.add)
-        nc.vector.tensor_tensor(out=res_pad[:, 0:B_TILES], in0=summed[:], in1=acc_ln[:], op=ALU.add)
+        partial = keep.tile([P, B_TILES], F32)
+        nc.vector.tensor_reduce(out=partial[:], in_=acc_abs[:], axis=AXIS.X, op=ALU.add)
+        nc.vector.tensor_tensor(out=partial[:], in0=acc_xv[:], in1=partial[:], op=ALU.subtract)
+        nc.vector.tensor_tensor(out=res_pad[:, 0:B_TILES], in0=partial[:], in1=acc_ln[:], op=ALU.add)
         resT_bank = psum.tile([P, P], F32, tag="bank")
         nc.tensor.transpose(resT_bank[:], res_pad[:], ident_f32[:])
         res_rows = keep.tile([B_TILES, P], F32)

@@ -96,7 +96,6 @@ def tile_gmvae_pb_s_kernel(tc, dec_h1, x, dw2, db2, dw3, db3, out):
         w2_grouped = keep.tile([P, HIDDEN, PACK], BF16, align_bytes=64)
         w2_halves = [slice(0, HIDDEN // 2), slice(HIDDEN // 2, HIDDEN)]
         regroup(nc.vector.tensor_copy, w2_grouped[:, w2_halves[0], :], w2_rows[:, :, w2_halves[0]])
-        regroup(nc.scalar.copy, w2_grouped[:, w2_halves[1], :], w2_rows[:, :, w2_halves[1]])
         b2_bank = psum.tile([P, P], BF16, tag="bank")
         nc.tensor.transpose(b2_bank[:], b2_rows[:], ident_bf16[:])
         b2 = keep.tile([P, PACK], F32)
@@ -106,23 +105,23 @@ def tile_gmvae_pb_s_kernel(tc, dec_h1, x, dw2, db2, dw3, db3, out):
         quantise(nc, a_grouped[:], a_codes[:], a_scales[:])
         w2_codes = keep.tile([P, HIDDEN], U32, align_bytes=64)
         w2_scales = keep.tile([P, HIDDEN], U8, align_bytes=64)
-        for h_half in w2_halves:
-            quantise(nc, w2_grouped[:, h_half, :], w2_codes[:, h_half], w2_scales[:, h_half])
+        quantise(nc, w2_grouped[:, w2_halves[0], :], w2_codes[:, w2_halves[0]], w2_scales[:, w2_halves[0]])
+        regroup(nc.vector.tensor_copy, w2_grouped[:, w2_halves[1], :], w2_rows[:, :, w2_halves[1]])
+        quantise(nc, w2_grouped[:, w2_halves[1], :], w2_codes[:, w2_halves[1]], w2_scales[:, w2_halves[1]])
 
         z_banks = []
-        for half in range(2):
-            z_bank = psum.tile([P, 2, BATCH], F32, tag="bank")
-            for s in range(2):
-                h_cols = slice((2 * half + s) * P, (2 * half + s + 1) * P)
-                nc.tensor.matmul_mx(
-                    out=z_bank[:, s, :],
-                    lhsT=w2_codes[:, h_cols].bitcast(FP8X4),
-                    lhsT_scale=w2_scales[:, h_cols],
-                    rhs=a_codes[:].bitcast(FP8X4),
-                    rhs_scale=a_scales[:],
-                    start=True,
-                    stop=True,
-                )
+        for t in range(PACK):
+            z_bank = psum.tile([P, BATCH], F32, tag="bank")
+            h_cols = slice(t * P, (t + 1) * P)
+            nc.tensor.matmul_mx(
+                out=z_bank[:],
+                lhsT=w2_codes[:, h_cols].bitcast(FP8X4),
+                lhsT_scale=w2_scales[:, h_cols],
+                rhs=a_codes[:].bitcast(FP8X4),
+                rhs_scale=a_scales[:],
+                start=True,
+                stop=True,
+            )
             z_banks.append(z_bank)
 
         w3_grouped = []
@@ -131,37 +130,30 @@ def tile_gmvae_pb_s_kernel(tc, dec_h1, x, dw2, db2, dw3, db3, out):
             w3_grouped.append(grouped)
         w3_codes = keep.tile([P, J_HALVES, BANK], U32, align_bytes=64)
         w3_scales = keep.tile([P, J_HALVES, BANK], U8, align_bytes=64)
+        vector_part = slice(0, BANK // 2)
+        scalar_part = slice(BANK // 2, BANK)
         regroup(nc.vector.tensor_copy, w3_grouped[0][:], w3_rows[0][:])
+        regroup(nc.vector.tensor_copy, w3_grouped[1][:, vector_part, :], w3_rows[1][:, :, vector_part])
+        quantise(nc, w3_grouped[0][:], w3_codes[:, 0, :], w3_scales[:, 0, :])
 
-        neg = keep.tile([P, PACK, BATCH], F32)
-        d2_rows = keep.tile([P, PACK, BATCH], BF16)
-        for half in range(2):
-            pair = slice(2 * half, 2 * half + 2)
-            for s in range(2):
-                t = 2 * half + s
-                nc.scalar.activation(
-                    out=neg[:, t, :], in_=z_banks[half][:, s, :], func=ACT.Exp, bias=b2[:, t : t + 1], scale=1.0
-                )
-            nc.vector.tensor_scalar(
-                out=neg[:, pair, :], in0=neg[:, pair, :], scalar1=-1.0, scalar2=0.0, op0=ALU.add, op1=ALU.min
-            )
-            for s in range(2):
-                t = 2 * half + s
-                nc.vector.scalar_tensor_tensor(
-                    out=d2_rows[:, t, :],
-                    in0=z_banks[half][:, s, :],
-                    scalar=b2[:, t : t + 1],
-                    in1=neg[:, t, :],
-                    op0=ALU.add,
-                    op1=ALU.max,
-                )
-        regroup(nc.scalar.copy, w3_grouped[1][:], w3_rows[1][:])
+        exp_y = keep.tile([P, PACK, BATCH], F32)
+        relu_y = keep.tile([P, PACK, BATCH], F32)
+        for t in range(PACK):
+            for term, func in ((exp_y, ACT.Exp), (relu_y, ACT.Relu)):
+                nc.scalar.activation(out=term[:, t, :], in_=z_banks[t][:], func=func, bias=b2[:, t : t + 1], scale=1.0)
+        regroup(nc.scalar.copy, w3_grouped[1][:, scalar_part, :], w3_rows[1][:, :, scalar_part])
         nc.scalar.activation(out=warm[:], in_=warm[:], func=ACT.Sigmoid)
         d2_grouped = keep.tile([P, BATCH, PACK], BF16, align_bytes=64)
         b_tiles = [slice(i * P, (i + 1) * P) for i in range(B_TILES)]
         for b_cols in b_tiles:
-            regroup(nc.vector.tensor_copy, d2_grouped[:, b_cols, :], d2_rows[:, :, b_cols])
-        quantise(nc, w3_grouped[0][:], w3_codes[:, 0, :], w3_scales[:, 0, :])
+            nc.vector.scalar_tensor_tensor(
+                out=d2_grouped[:, b_cols, :],
+                in0=exp_y[:, :, b_cols].rearrange("p t b -> p b t"),
+                scalar=-1.0,
+                in1=relu_y[:, :, b_cols].rearrange("p t b -> p b t"),
+                op0=ALU.add,
+                op1=ALU.min,
+            )
         d2_codes = keep.tile([P, BATCH], U32, align_bytes=64)
         d2_scales = keep.tile([P, BATCH], U8, align_bytes=64)
         for b_cols in b_tiles:

@@ -21,6 +21,7 @@ B_TILES = BATCH // P
 BANK = 512
 J_HALVES = PIXELS // BANK
 RUN = 4
+BLOCK = 32
 FACTORS = 32
 
 FLOPS = 2 * BATCH * HIDDEN * HIDDEN + 2 * BATCH * HIDDEN * PIXELS
@@ -53,7 +54,7 @@ def tile_gmvae_pb_s_kernel(tc, dec_h1, x, dw2, db2, dw3, db3, out):
         nc.gpsimd.memset(b2_rows[:], 0.0)
         warm = keep.tile([P, 1], F32)
         nc.vector.memset(warm[:], 0.0)
-        res_pad = keep.tile([P, P], F32)
+        res_pad = keep.tile([P, BLOCK], F32, align_bytes=64)
         nc.vector.memset(res_pad[:], 0.0)
         ident_f32 = keep.tile([P, P], F32)
         make_identity(nc, ident_f32[:])
@@ -96,6 +97,7 @@ def tile_gmvae_pb_s_kernel(tc, dec_h1, x, dw2, db2, dw3, db3, out):
         w2_grouped = keep.tile([P, HIDDEN, PACK], BF16, align_bytes=64)
         w2_halves = [slice(0, HIDDEN // 2), slice(HIDDEN // 2, HIDDEN)]
         regroup(nc.vector.tensor_copy, w2_grouped[:, w2_halves[0], :], w2_rows[:, :, w2_halves[0]])
+        regroup(nc.scalar.copy, w2_grouped[:, w2_halves[1], :], w2_rows[:, :, w2_halves[1]])
         b2_bank = psum.tile([P, P], BF16, tag="bank")
         nc.tensor.transpose(b2_bank[:], b2_rows[:], ident_bf16[:])
         b2 = keep.tile([P, PACK], F32)
@@ -106,7 +108,13 @@ def tile_gmvae_pb_s_kernel(tc, dec_h1, x, dw2, db2, dw3, db3, out):
         w2_codes = keep.tile([P, HIDDEN], U32, align_bytes=64)
         w2_scales = keep.tile([P, HIDDEN], U8, align_bytes=64)
         quantise(nc, w2_grouped[:, w2_halves[0], :], w2_codes[:, w2_halves[0]], w2_scales[:, w2_halves[0]])
-        regroup(nc.vector.tensor_copy, w2_grouped[:, w2_halves[1], :], w2_rows[:, :, w2_halves[1]])
+        w3_grouped = []
+        for jh in range(J_HALVES):
+            grouped = keep.tile([P, BANK, PACK], BF16, align_bytes=64, name="w3_grouped%d" % jh)
+            w3_grouped.append(grouped)
+        first_part = slice(0, BANK // 2)
+        second_part = slice(BANK // 2, BANK)
+        regroup(nc.vector.tensor_copy, w3_grouped[0][:, first_part, :], w3_rows[0][:, :, first_part])
         quantise(nc, w2_grouped[:, w2_halves[1], :], w2_codes[:, w2_halves[1]], w2_scales[:, w2_halves[1]])
 
         z_banks = []
@@ -124,16 +132,10 @@ def tile_gmvae_pb_s_kernel(tc, dec_h1, x, dw2, db2, dw3, db3, out):
             )
             z_banks.append(z_bank)
 
-        w3_grouped = []
-        for jh in range(J_HALVES):
-            grouped = keep.tile([P, BANK, PACK], BF16, align_bytes=64, name="w3_grouped%d" % jh)
-            w3_grouped.append(grouped)
         w3_codes = keep.tile([P, J_HALVES, BANK], U32, align_bytes=64)
         w3_scales = keep.tile([P, J_HALVES, BANK], U8, align_bytes=64)
-        vector_part = slice(0, BANK // 2)
-        scalar_part = slice(BANK // 2, BANK)
-        regroup(nc.vector.tensor_copy, w3_grouped[0][:], w3_rows[0][:])
-        regroup(nc.vector.tensor_copy, w3_grouped[1][:, vector_part, :], w3_rows[1][:, :, vector_part])
+        regroup(nc.vector.tensor_copy, w3_grouped[0][:, second_part, :], w3_rows[0][:, :, second_part])
+        regroup(nc.vector.tensor_copy, w3_grouped[1][:, first_part, :], w3_rows[1][:, :, first_part])
         quantise(nc, w3_grouped[0][:], w3_codes[:, 0, :], w3_scales[:, 0, :])
 
         exp_y = keep.tile([P, PACK, BATCH], F32)
@@ -141,7 +143,7 @@ def tile_gmvae_pb_s_kernel(tc, dec_h1, x, dw2, db2, dw3, db3, out):
         for t in range(PACK):
             for term, func in ((exp_y, ACT.Exp), (relu_y, ACT.Relu)):
                 nc.scalar.activation(out=term[:, t, :], in_=z_banks[t][:], func=func, bias=b2[:, t : t + 1], scale=1.0)
-        regroup(nc.scalar.copy, w3_grouped[1][:, scalar_part, :], w3_rows[1][:, :, scalar_part])
+        regroup(nc.scalar.copy, w3_grouped[1][:, second_part, :], w3_rows[1][:, :, second_part])
         nc.scalar.activation(out=warm[:], in_=warm[:], func=ACT.Sigmoid)
         d2_grouped = keep.tile([P, BATCH, PACK], BF16, align_bytes=64)
         b_tiles = [slice(i * P, (i + 1) * P) for i in range(B_TILES)]
@@ -197,6 +199,8 @@ def tile_gmvae_pb_s_kernel(tc, dec_h1, x, dw2, db2, dw3, db3, out):
             )
         products = keep.tile([P, B_TILES, PIXELS // FACTORS], F32)
         acc_ln = keep.tile([P, B_TILES], F32)
+        sum_abs = keep.tile([P, B_TILES], F32)
+        partial = keep.tile([P, B_TILES], F32)
         for i in range(B_TILES):
             nc.vector.tensor_reduce(
                 out=products[:, i, :],
@@ -205,13 +209,13 @@ def tile_gmvae_pb_s_kernel(tc, dec_h1, x, dw2, db2, dw3, db3, out):
                 op=ALU.mult,
             )
             nc.scalar.activation(out=products[:, i, :], in_=products[:, i, :], func=ACT.Ln, accum_out=acc_ln[:, i : i + 1])
+            if i == 0:
+                nc.vector.tensor_reduce(out=sum_abs[:], in_=acc_abs[:], axis=AXIS.X, op=ALU.add)
+        nc.vector.tensor_tensor(out=partial[:], in0=acc_xv[:], in1=sum_abs[:], op=ALU.subtract)
 
-        partial = keep.tile([P, B_TILES], F32)
-        nc.vector.tensor_reduce(out=partial[:], in_=acc_abs[:], axis=AXIS.X, op=ALU.add)
-        nc.vector.tensor_tensor(out=partial[:], in0=acc_xv[:], in1=partial[:], op=ALU.subtract)
         nc.vector.tensor_tensor(out=res_pad[:, 0:B_TILES], in0=partial[:], in1=acc_ln[:], op=ALU.add)
-        resT_bank = psum.tile([P, P], F32, tag="bank")
-        nc.tensor.transpose(resT_bank[:], res_pad[:], ident_f32[:])
-        res_rows = keep.tile([B_TILES, P], F32)
-        nc.vector.tensor_copy(out=res_rows[:], in_=resT_bank[0:B_TILES, :])
-        nc.sync.dma_start(out=out.rearrange("(i p) -> i p", p=P), in_=res_rows[:])
+        res_rows = keep.tile([P, BLOCK], F32, align_bytes=64)
+        nc.vector.transpose(res_rows[:], res_pad[:])
+        out_rows = out.rearrange("(i q c) -> i q c", i=B_TILES, c=BLOCK)
+        for i in range(B_TILES):
+            nc.sync.dma_start(out=out_rows[i], in_=res_rows[i : P : BLOCK, :])

@@ -114,7 +114,6 @@ def tile_gmvae_pb_s_kernel(tc, dec_h1, x, dw2, db2, dw3, db3, out):
             w3_grouped.append(grouped)
         first_part = slice(0, BANK // 2)
         second_part = slice(BANK // 2, BANK)
-        regroup(nc.vector.tensor_copy, w3_grouped[0][:, first_part, :], w3_rows[0][:, :, first_part])
         quantise(nc, w2_grouped[:, w2_halves[1], :], w2_codes[:, w2_halves[1]], w2_scales[:, w2_halves[1]])
 
         z_banks = []
@@ -134,7 +133,7 @@ def tile_gmvae_pb_s_kernel(tc, dec_h1, x, dw2, db2, dw3, db3, out):
 
         w3_codes = keep.tile([P, J_HALVES, BANK], U32, align_bytes=64)
         w3_scales = keep.tile([P, J_HALVES, BANK], U8, align_bytes=64)
-        regroup(nc.vector.tensor_copy, w3_grouped[0][:, second_part, :], w3_rows[0][:, :, second_part])
+        regroup(nc.vector.tensor_copy, w3_grouped[0][:], w3_rows[0][:])
         regroup(nc.vector.tensor_copy, w3_grouped[1][:, first_part, :], w3_rows[1][:, :, first_part])
         quantise(nc, w3_grouped[0][:], w3_codes[:, 0, :], w3_scales[:, 0, :])
 

@@ -63,7 +63,8 @@ def tile_gmvae_pb_s_kernel(tc, dec_h1, x, dw2, db2, dw3, db3, out):
         nc.scalar.activation(out=warm[:], in_=warm[:], func=ACT.Exp)
 
         a_rows = keep.tile([P, B_TILES, HIDDEN], BF16)
-        nc.sync.dma_start(out=a_rows[:], in_=dec_h1.rearrange("(i p) k -> p i k", p=P))
+        for i in range(B_TILES):
+            nc.sync.dma_start(out=a_rows[:, i, :], in_=dec_h1[i * P : (i + 1) * P, :])
         nc.sync.dma_start(out=b2_rows[0:PACK, :], in_=db2.rearrange("(t p) -> t p", p=P))
         w2_rows = keep.tile([P, PACK, HIDDEN], BF16)
         nc.sync.dma_start(
@@ -84,19 +85,19 @@ def tile_gmvae_pb_s_kernel(tc, dec_h1, x, dw2, db2, dw3, db3, out):
         nc.sync.dma_start(out=x_rows[:], in_=x.rearrange("(i p) j -> p i j", p=P))
 
         a_words = a_rows[:].bitcast(F32)
-        aT_bank = psum.tile([P, 2, BATCH], F32, tag="bank")
-        for u in range(2):
-            for i in range(B_TILES):
-                nc.tensor.transpose(
-                    aT_bank[:, u, i * P : (i + 1) * P], a_words[:, i, u * P : (u + 1) * P], ident_f32[:]
-                )
         a_grouped = keep.tile([P, BATCH, PACK], BF16, align_bytes=64)
-        nc.scalar.copy(out=a_grouped[:].bitcast(F32), in_=aT_bank[:].rearrange("p u b -> p b u"))
-
+        a_grouped_words = a_grouped[:].rearrange("p b t -> p (b t)").bitcast(F32).rearrange("p (b u) -> p b u", u=2)
+        b_tiles = [slice(i * P, (i + 1) * P) for i in range(B_TILES)]
+        for i in range(B_TILES):
+            aT_bank = psum.tile([P, 2, P], F32, tag="bank")
+            for u in range(2):
+                nc.tensor.transpose(aT_bank[:, u, :], a_words[:, i, u * P : (u + 1) * P], ident_f32[:])
+            nc.scalar.copy(out=a_grouped_words[:, b_tiles[i], :], in_=aT_bank[:].rearrange("p u b -> p b u"))
 
         w2_grouped = keep.tile([P, HIDDEN, PACK], BF16, align_bytes=64)
         w2_halves = [slice(0, HIDDEN // 2), slice(HIDDEN // 2, HIDDEN)]
-        regroup(nc.vector.tensor_copy, w2_grouped[:, w2_halves[0], :], w2_rows[:, :, w2_halves[0]])
+        w2_quarters = [slice(q * P, (q + 1) * P) for q in range(2)]
+        regroup(nc.vector.tensor_copy, w2_grouped[:, w2_quarters[0], :], w2_rows[:, :, w2_quarters[0]])
         regroup(nc.scalar.copy, w2_grouped[:, w2_halves[1], :], w2_rows[:, :, w2_halves[1]])
         b2_bank = psum.tile([P, P], BF16, tag="bank")
         nc.tensor.transpose(b2_bank[:], b2_rows[:], ident_bf16[:])
@@ -107,13 +108,13 @@ def tile_gmvae_pb_s_kernel(tc, dec_h1, x, dw2, db2, dw3, db3, out):
         quantise(nc, a_grouped[:], a_codes[:], a_scales[:])
         w2_codes = keep.tile([P, HIDDEN], U32, align_bytes=64)
         w2_scales = keep.tile([P, HIDDEN], U8, align_bytes=64)
-        quantise(nc, w2_grouped[:, w2_halves[0], :], w2_codes[:, w2_halves[0]], w2_scales[:, w2_halves[0]])
+        quantise(nc, w2_grouped[:, w2_quarters[0], :], w2_codes[:, w2_quarters[0]], w2_scales[:, w2_quarters[0]])
+        regroup(nc.vector.tensor_copy, w2_grouped[:, w2_quarters[1], :], w2_rows[:, :, w2_quarters[1]])
+        quantise(nc, w2_grouped[:, w2_quarters[1], :], w2_codes[:, w2_quarters[1]], w2_scales[:, w2_quarters[1]])
         w3_grouped = []
         for jh in range(J_HALVES):
             grouped = keep.tile([P, BANK, PACK], BF16, align_bytes=64, name="w3_grouped%d" % jh)
             w3_grouped.append(grouped)
-        first_part = slice(0, BANK // 2)
-        second_part = slice(BANK // 2, BANK)
         quantise(nc, w2_grouped[:, w2_halves[1], :], w2_codes[:, w2_halves[1]], w2_scales[:, w2_halves[1]])
 
         z_banks = []
@@ -133,19 +134,25 @@ def tile_gmvae_pb_s_kernel(tc, dec_h1, x, dw2, db2, dw3, db3, out):
 
         w3_codes = keep.tile([P, J_HALVES, BANK], U32, align_bytes=64)
         w3_scales = keep.tile([P, J_HALVES, BANK], U8, align_bytes=64)
+        vector_part = slice(0, BANK // 4)
+        scalar_part = slice(BANK // 4, BANK)
         regroup(nc.vector.tensor_copy, w3_grouped[0][:], w3_rows[0][:])
-        regroup(nc.vector.tensor_copy, w3_grouped[1][:, first_part, :], w3_rows[1][:, :, first_part])
-        quantise(nc, w3_grouped[0][:], w3_codes[:, 0, :], w3_scales[:, 0, :])
 
         exp_y = keep.tile([P, PACK, BATCH], F32)
         relu_y = keep.tile([P, PACK, BATCH], F32)
+        last_t = PACK - 1
+        nc.vector.tensor_scalar(
+            out=relu_y[:, last_t, :], in0=z_banks[last_t][:], scalar1=b2[:, last_t:PACK], scalar2=0.0, op0=ALU.add, op1=ALU.max
+        )
+        regroup(nc.vector.tensor_copy, w3_grouped[1][:, vector_part, :], w3_rows[1][:, :, vector_part])
+        quantise(nc, w3_grouped[0][:], w3_codes[:, 0, :], w3_scales[:, 0, :])
         for t in range(PACK):
-            for term, func in ((exp_y, ACT.Exp), (relu_y, ACT.Relu)):
-                nc.scalar.activation(out=term[:, t, :], in_=z_banks[t][:], func=func, bias=b2[:, t : t + 1], scale=1.0)
-        regroup(nc.scalar.copy, w3_grouped[1][:, second_part, :], w3_rows[1][:, :, second_part])
+            nc.scalar.activation(out=exp_y[:, t, :], in_=z_banks[t][:], func=ACT.Exp, bias=b2[:, t : t + 1], scale=1.0)
+            if t < last_t:
+                nc.scalar.activation(out=relu_y[:, t, :], in_=z_banks[t][:], func=ACT.Relu, bias=b2[:, t : t + 1], scale=1.0)
+        regroup(nc.scalar.copy, w3_grouped[1][:, scalar_part, :], w3_rows[1][:, :, scalar_part])
         nc.scalar.activation(out=warm[:], in_=warm[:], func=ACT.Sigmoid)
         d2_grouped = keep.tile([P, BATCH, PACK], BF16, align_bytes=64)
-        b_tiles = [slice(i * P, (i + 1) * P) for i in range(B_TILES)]
         for b_cols in b_tiles:
             nc.vector.scalar_tensor_tensor(
                 out=d2_grouped[:, b_cols, :],
@@ -163,25 +170,27 @@ def tile_gmvae_pb_s_kernel(tc, dec_h1, x, dw2, db2, dw3, db3, out):
 
         v_all = keep.tile([P, B_TILES, PIXELS], F32)
         sig = keep.tile([P, B_TILES, PIXELS], F32)
-        acc_abs = keep.tile([P, B_TILES, J_HALVES], F32)
-        for jh in range(J_HALVES):
-            cols = slice(jh * BANK, (jh + 1) * BANK)
-            for i in range(B_TILES):
-                logit_bank = psum.tile([P, BANK], F32, tag="bank")
-                nc.tensor.matmul_mx(
-                    out=logit_bank[:],
-                    lhsT=d2_codes[:, b_tiles[i]].bitcast(FP8X4),
-                    lhsT_scale=d2_scales[:, b_tiles[i]],
-                    rhs=w3_codes[:, jh, :].bitcast(FP8X4),
-                    rhs_scale=w3_scales[:, jh, :],
-                    start=True,
-                    stop=True,
-                )
-                nc.vector.tensor_tensor(out=v_all[:, i, cols], in0=logit_bank[:], in1=b3_all[:, cols], op=ALU.add)
-                nc.scalar.activation(
-                    out=sig[:, i, cols], in_=v_all[:, i, cols], func=ACT.Abs, scale=0.5, accum_out=acc_abs[:, i, jh : jh + 1]
-                )
-                nc.scalar.activation(out=sig[:, i, cols], in_=sig[:, i, cols], func=ACT.Sigmoid, scale=2.0)
+        pieces = [(0, 0, 0, BANK // 2), (0, 0, BANK // 2, BANK), (0, 1, 0, BANK), (1, 0, 0, BANK), (1, 1, 0, BANK)]
+        acc_abs = keep.tile([P, B_TILES, len(pieces) - B_TILES], F32)
+        nc.gpsimd.memset(acc_abs[:], 0.0)
+        for n, (jh, i, first, last) in enumerate(pieces):
+            cols = slice(jh * BANK + first, jh * BANK + last)
+            logit_bank = psum.tile([P, last - first], F32, tag="bank")
+            nc.tensor.matmul_mx(
+                out=logit_bank[:],
+                lhsT=d2_codes[:, b_tiles[i]].bitcast(FP8X4),
+                lhsT_scale=d2_scales[:, b_tiles[i]],
+                rhs=w3_codes[:, jh, first:last].bitcast(FP8X4),
+                rhs_scale=w3_scales[:, jh, first:last],
+                start=True,
+                stop=True,
+            )
+            nc.vector.tensor_tensor(out=v_all[:, i, cols], in0=logit_bank[:], in1=b3_all[:, cols], op=ALU.add)
+            slot = jh if i else jh + (n > 0)
+            nc.scalar.activation(
+                out=sig[:, i, cols], in_=v_all[:, i, cols], func=ACT.Abs, scale=0.5, accum_out=acc_abs[:, i, slot : slot + 1]
+            )
+            nc.scalar.activation(out=sig[:, i, cols], in_=sig[:, i, cols], func=ACT.Sigmoid, scale=2.0)
         nc.scalar.activation(out=warm[:], in_=warm[:], func=ACT.Ln)
 
         acc_xv = keep.tile([P, B_TILES], F32)

@@ -60,6 +60,10 @@ def tile_gmvae_pb_s_kernel(tc, dec_h1, x, dw2, db2, dw3, db3, out):
         make_identity(nc, ident_f32[:])
         ident_bf16 = keep.tile([P, P], BF16)
         make_identity(nc, ident_bf16[:])
+        b3_row = keep.tile([P, PIXELS], BF16)
+        nc.vector.memset(b3_row[:], 0.0)
+        ones = keep.tile([P, P], BF16)
+        nc.vector.memset(ones[:], 1.0)
         nc.scalar.activation(out=warm[:], in_=warm[:], func=ACT.Exp)
 
         a_rows = keep.tile([P, B_TILES, HIDDEN], BF16)
@@ -79,8 +83,7 @@ def tile_gmvae_pb_s_kernel(tc, dec_h1, x, dw2, db2, dw3, db3, out):
                 in_=dw3[:, jh * BANK : (jh + 1) * BANK].rearrange("(t p) j -> p t j", p=P),
             )
             w3_rows.append(rows)
-        b3_all = keep.tile([P, PIXELS], BF16)
-        nc.sync.dma_start(out=b3_all[:], in_=db3.partition_broadcast(P))
+        nc.sync.dma_start(out=b3_row[0:1, :], in_=db3.rearrange("(o j) -> o j", o=1))
         x_rows = keep.tile([P, B_TILES, PIXELS], BF16)
         nc.sync.dma_start(out=x_rows[:], in_=x.rearrange("(i p) j -> p i j", p=P))
 
@@ -132,10 +135,16 @@ def tile_gmvae_pb_s_kernel(tc, dec_h1, x, dw2, db2, dw3, db3, out):
             )
             z_banks.append(z_bank)
 
+        b3_bank = psum.tile([P, PIXELS], BF16, tag="bank")
+        for jh in range(J_HALVES):
+            cols = slice(jh * BANK, (jh + 1) * BANK)
+            nc.tensor.matmul(b3_bank[:, cols], lhsT=ones[:], rhs=b3_row[:, cols], start=True, stop=True)
+        b3_all = keep.tile([P, PIXELS], BF16)
+
         w3_codes = keep.tile([P, J_HALVES, BANK], U32, align_bytes=64)
         w3_scales = keep.tile([P, J_HALVES, BANK], U8, align_bytes=64)
-        vector_part = slice(0, BANK // 4)
-        scalar_part = slice(BANK // 4, BANK)
+        vector_part = slice(0, BANK // 2)
+        scalar_part = slice(BANK // 2, BANK)
         regroup(nc.vector.tensor_copy, w3_grouped[0][:], w3_rows[0][:])
 
         exp_y = keep.tile([P, PACK, BATCH], F32)
@@ -150,6 +159,7 @@ def tile_gmvae_pb_s_kernel(tc, dec_h1, x, dw2, db2, dw3, db3, out):
             nc.scalar.activation(out=exp_y[:, t, :], in_=z_banks[t][:], func=ACT.Exp, bias=b2[:, t : t + 1], scale=1.0)
             if t < last_t:
                 nc.scalar.activation(out=relu_y[:, t, :], in_=z_banks[t][:], func=ACT.Relu, bias=b2[:, t : t + 1], scale=1.0)
+        nc.scalar.copy(out=b3_all[:], in_=b3_bank[:])
         regroup(nc.scalar.copy, w3_grouped[1][:, scalar_part, :], w3_rows[1][:, :, scalar_part])
         nc.scalar.activation(out=warm[:], in_=warm[:], func=ACT.Sigmoid)
         d2_grouped = keep.tile([P, BATCH, PACK], BF16, align_bytes=64)

@@ -61,7 +61,7 @@ def tile_gmvae_pb_s_kernel(tc, dec_h1, x, dw2, db2, dw3, db3, out):
         ident_bf16 = keep.tile([P, P], BF16)
         make_identity(nc, ident_bf16[:])
         b3_row = keep.tile([P, PIXELS], BF16)
-        nc.vector.memset(b3_row[:], 0.0)
+        nc.vector.memset(b3_row[:].bitcast(F32), 0.0)
         ones = keep.tile([P, P], BF16)
         nc.vector.memset(ones[:], 1.0)
         nc.scalar.activation(out=warm[:], in_=warm[:], func=ACT.Exp)
@@ -70,6 +70,7 @@ def tile_gmvae_pb_s_kernel(tc, dec_h1, x, dw2, db2, dw3, db3, out):
         for i in range(B_TILES):
             nc.sync.dma_start(out=a_rows[:, i, :], in_=dec_h1[i * P : (i + 1) * P, :])
         nc.sync.dma_start(out=b2_rows[0:PACK, :], in_=db2.rearrange("(t p) -> t p", p=P))
+        nc.sync.dma_start(out=b3_row[0:1, :], in_=db3.rearrange("(o j) -> o j", o=1))
         w2_rows = keep.tile([P, PACK, HIDDEN], BF16)
         nc.sync.dma_start(
             out=w2_rows[:].rearrange("p (u e) h -> p u e h", u=2),
@@ -83,7 +84,6 @@ def tile_gmvae_pb_s_kernel(tc, dec_h1, x, dw2, db2, dw3, db3, out):
                 in_=dw3[:, jh * BANK : (jh + 1) * BANK].rearrange("(t p) j -> p t j", p=P),
             )
             w3_rows.append(rows)
-        nc.sync.dma_start(out=b3_row[0:1, :], in_=db3.rearrange("(o j) -> o j", o=1))
         x_rows = keep.tile([P, B_TILES, PIXELS], BF16)
         nc.sync.dma_start(out=x_rows[:], in_=x.rearrange("(i p) j -> p i j", p=P))
 
@@ -106,6 +106,12 @@ def tile_gmvae_pb_s_kernel(tc, dec_h1, x, dw2, db2, dw3, db3, out):
         nc.tensor.transpose(b2_bank[:], b2_rows[:], ident_bf16[:])
         b2 = keep.tile([P, PACK], F32)
         nc.scalar.copy(out=b2[:], in_=b2_bank[:, 0:PACK])
+        b3_bank = psum.tile([P, PIXELS], BF16, tag="bank")
+        for jh in range(J_HALVES):
+            cols = slice(jh * BANK, (jh + 1) * BANK)
+            nc.tensor.matmul(b3_bank[:, cols], lhsT=ones[:], rhs=b3_row[:, cols], start=True, stop=True)
+        b3_all = keep.tile([P, PIXELS], BF16)
+        nc.scalar.copy(out=b3_all[:], in_=b3_bank[:])
         a_codes = keep.tile([P, BATCH], U32, align_bytes=64)
         a_scales = keep.tile([P, BATCH], U8, align_bytes=64)
         quantise(nc, a_grouped[:], a_codes[:], a_scales[:])
@@ -135,12 +141,6 @@ def tile_gmvae_pb_s_kernel(tc, dec_h1, x, dw2, db2, dw3, db3, out):
             )
             z_banks.append(z_bank)
 
-        b3_bank = psum.tile([P, PIXELS], BF16, tag="bank")
-        for jh in range(J_HALVES):
-            cols = slice(jh * BANK, (jh + 1) * BANK)
-            nc.tensor.matmul(b3_bank[:, cols], lhsT=ones[:], rhs=b3_row[:, cols], start=True, stop=True)
-        b3_all = keep.tile([P, PIXELS], BF16)
-
         w3_codes = keep.tile([P, J_HALVES, BANK], U32, align_bytes=64)
         w3_scales = keep.tile([P, J_HALVES, BANK], U8, align_bytes=64)
         vector_part = slice(0, BANK // 2)
@@ -159,7 +159,6 @@ def tile_gmvae_pb_s_kernel(tc, dec_h1, x, dw2, db2, dw3, db3, out):
             nc.scalar.activation(out=exp_y[:, t, :], in_=z_banks[t][:], func=ACT.Exp, bias=b2[:, t : t + 1], scale=1.0)
             if t < last_t:
                 nc.scalar.activation(out=relu_y[:, t, :], in_=z_banks[t][:], func=ACT.Relu, bias=b2[:, t : t + 1], scale=1.0)
-        nc.scalar.copy(out=b3_all[:], in_=b3_bank[:])
         regroup(nc.scalar.copy, w3_grouped[1][:, scalar_part, :], w3_rows[1][:, :, scalar_part])
         nc.scalar.activation(out=warm[:], in_=warm[:], func=ACT.Sigmoid)
         d2_grouped = keep.tile([P, BATCH, PACK], BF16, align_bytes=64)

@@ -52,6 +52,8 @@ def tile_gmvae_pb_s_kernel(tc, dec_h1, x, dw2, db2, dw3, db3, out):
 
         b2_rows = keep.tile([P, P], BF16)
         nc.gpsimd.memset(b2_rows[:], 0.0)
+        b3_row = keep.tile([P, PIXELS], BF16)
+        nc.vector.memset(b3_row[:].bitcast(F32), 0.0)
         warm = keep.tile([P, 1], F32)
         nc.vector.memset(warm[:], 0.0)
         res_pad = keep.tile([P, BLOCK], F32, align_bytes=64)
@@ -60,8 +62,6 @@ def tile_gmvae_pb_s_kernel(tc, dec_h1, x, dw2, db2, dw3, db3, out):
         make_identity(nc, ident_f32[:])
         ident_bf16 = keep.tile([P, P], BF16)
         make_identity(nc, ident_bf16[:])
-        b3_row = keep.tile([P, PIXELS], BF16)
-        nc.vector.memset(b3_row[:].bitcast(F32), 0.0)
         ones = keep.tile([P, P], BF16)
         nc.vector.memset(ones[:], 1.0)
         nc.scalar.activation(out=warm[:], in_=warm[:], func=ACT.Exp)
@@ -69,13 +69,13 @@ def tile_gmvae_pb_s_kernel(tc, dec_h1, x, dw2, db2, dw3, db3, out):
         a_rows = keep.tile([P, B_TILES, HIDDEN], BF16)
         for i in range(B_TILES):
             nc.sync.dma_start(out=a_rows[:, i, :], in_=dec_h1[i * P : (i + 1) * P, :])
-        nc.sync.dma_start(out=b2_rows[0:PACK, :], in_=db2.rearrange("(t p) -> t p", p=P))
-        nc.sync.dma_start(out=b3_row[0:1, :], in_=db3.rearrange("(o j) -> o j", o=1))
         w2_rows = keep.tile([P, PACK, HIDDEN], BF16)
         nc.sync.dma_start(
             out=w2_rows[:].rearrange("p (u e) h -> p u e h", u=2),
             in_=dw2.rearrange("(u p e) h -> p u e h", u=2, e=2),
         )
+        nc.sync.dma_start(out=b2_rows[0:PACK, :], in_=db2.rearrange("(t p) -> t p", p=P))
+        nc.sync.dma_start(out=b3_row[0:1, :], in_=db3.rearrange("(o j) -> o j", o=1))
         w3_rows = []
         for jh in range(J_HALVES):
             rows = keep.tile([P, PACK, BANK], BF16, name="w3_rows%d" % jh)

@@ -143,8 +143,8 @@ def tile_gmvae_pb_s_kernel(tc, dec_h1, x, dw2, db2, dw3, db3, out):
 
         w3_codes = keep.tile([P, J_HALVES, BANK], U32, align_bytes=64)
         w3_scales = keep.tile([P, J_HALVES, BANK], U8, align_bytes=64)
-        vector_part = slice(0, BANK // 2)
-        scalar_part = slice(BANK // 2, BANK)
+        vector_part = slice(0, BANK * 3 // 8)
+        scalar_part = slice(BANK * 3 // 8, BANK)
         regroup(nc.vector.tensor_copy, w3_grouped[0][:], w3_rows[0][:])
 
         exp_y = keep.tile([P, PACK, BATCH], F32)
@@ -234,5 +234,5 @@ def tile_gmvae_pb_s_kernel(tc, dec_h1, x, dw2, db2, dw3, db3, out):
         res_rows = keep.tile([P, BLOCK], F32, align_bytes=64)
         nc.vector.transpose(res_rows[:], res_pad[:])
         out_rows = out.rearrange("(i q c) -> i q c", i=B_TILES, c=BLOCK)
-        for i in range(B_TILES):
-            nc.sync.dma_start(out=out_rows[i], in_=res_rows[i : P : BLOCK, :])
+        for i, queue in enumerate((nc.sync, nc.scalar)):
+            queue.dma_start(out=out_rows[i], in_=res_rows[i : P : BLOCK, :])

from contextlib import ExitStack

import concourse.mybir as mybir
from concourse.masks import make_identity

F32 = mybir.dt.float32
BF16 = mybir.dt.bfloat16
U32 = mybir.dt.uint32
U8 = mybir.dt.uint8
FP8X4 = mybir.dt.float8_e4m3fn_x4
ALU = mybir.AluOpType
ACT = mybir.ActivationFunctionType
AXIS = mybir.AxisListType

P = 128
PACK = 4
BATCH = 256
HIDDEN = 512
PIXELS = 1024
B_TILES = BATCH // P
BANK = 512
J_HALVES = PIXELS // BANK
RUN = 4
BLOCK = 32
FACTORS = 32

FLOPS = 2 * BATCH * HIDDEN * HIDDEN + 2 * BATCH * HIDDEN * PIXELS


def regroup(copy, grouped, rows):
    copy(
        out=grouped.rearrange("p (c i) t -> p c t i", i=RUN),
        in_=rows.rearrange("p t (c i) -> p c t i", i=RUN),
    )


def quantise(nc, grouped, codes, scales):
    nc.vector.quantize_mx(
        out=codes.bitcast(FP8X4),
        scales=scales,
        in_=grouped.rearrange("p w t -> p (w t)"),
    )


def tile_gmvae_pb_s_kernel(tc, dec_h1, x, dw2, db2, dw3, db3, out):
    nc = tc.nc
    with ExitStack() as ctx:
        keep = ctx.enter_context(tc.tile_pool(name="keep", bufs=1))
        psum = ctx.enter_context(tc.psum_pool(name="psum", bufs=8))

        ctx.enter_context(tc.manual_schedule())

        b2_rows = keep.tile([P, P], BF16)
        nc.gpsimd.memset(b2_rows[:], 0.0)
        b3_row = keep.tile([P, PIXELS], BF16)
        nc.vector.memset(b3_row[:].bitcast(F32), 0.0)
        warm = keep.tile([P, 1], F32)
        nc.vector.memset(warm[:], 0.0)
        res_pad = keep.tile([P, BLOCK], F32, align_bytes=64)
        nc.vector.memset(res_pad[:], 0.0)
        ident_f32 = keep.tile([P, P], F32)
        make_identity(nc, ident_f32[:])
        ident_bf16 = keep.tile([P, P], BF16)
        make_identity(nc, ident_bf16[:])
        ones = keep.tile([P, P], BF16)
        nc.vector.memset(ones[:], 1.0)
        nc.scalar.activation(out=warm[:], in_=warm[:], func=ACT.Exp)

        a_rows = keep.tile([P, B_TILES, HIDDEN], BF16)
        for i in range(B_TILES):
            nc.sync.dma_start(out=a_rows[:, i, :], in_=dec_h1[i * P : (i + 1) * P, :])
        w2_rows = keep.tile([P, PACK, HIDDEN], BF16)
        nc.sync.dma_start(
            out=w2_rows[:].rearrange("p (u e) h -> p u e h", u=2),
            in_=dw2.rearrange("(u p e) h -> p u e h", u=2, e=2),
        )
        nc.sync.dma_start(out=b2_rows[0:PACK, :], in_=db2.rearrange("(t p) -> t p", p=P))
        nc.sync.dma_start(out=b3_row[0:1, :], in_=db3.rearrange("(o j) -> o j", o=1))
        w3_rows = []
        for jh in range(J_HALVES):
            rows = keep.tile([P, PACK, BANK], BF16, name="w3_rows%d" % jh)
            nc.sync.dma_start(
                out=rows[:],
                in_=dw3[:, jh * BANK : (jh + 1) * BANK].rearrange("(t p) j -> p t j", p=P),
            )
            w3_rows.append(rows)
        x_rows = keep.tile([P, B_TILES, PIXELS], BF16)
        nc.sync.dma_start(out=x_rows[:], in_=x.rearrange("(i p) j -> p i j", p=P))

        a_words = a_rows[:].bitcast(F32)
        a_grouped = keep.tile([P, BATCH, PACK], BF16, align_bytes=64)
        a_grouped_words = a_grouped[:].rearrange("p b t -> p (b t)").bitcast(F32).rearrange("p (b u) -> p b u", u=2)
        b_tiles = [slice(i * P, (i + 1) * P) for i in range(B_TILES)]
        for i in range(B_TILES):
            aT_bank = psum.tile([P, 2, P], F32, tag="bank")
            for u in range(2):
                nc.tensor.transpose(aT_bank[:, u, :], a_words[:, i, u * P : (u + 1) * P], ident_f32[:])
            nc.scalar.copy(out=a_grouped_words[:, b_tiles[i], :], in_=aT_bank[:].rearrange("p u b -> p b u"))

        w2_grouped = keep.tile([P, HIDDEN, PACK], BF16, align_bytes=64)
        w2_halves = [slice(0, HIDDEN // 2), slice(HIDDEN // 2, HIDDEN)]
        w2_quarters = [slice(q * P, (q + 1) * P) for q in range(2)]
        regroup(nc.vector.tensor_copy, w2_grouped[:, w2_quarters[0], :], w2_rows[:, :, w2_quarters[0]])
        regroup(nc.scalar.copy, w2_grouped[:, w2_halves[1], :], w2_rows[:, :, w2_halves[1]])
        b2_bank = psum.tile([P, P], BF16, tag="bank")
        nc.tensor.transpose(b2_bank[:], b2_rows[:], ident_bf16[:])
        b2 = keep.tile([P, PACK], F32)
        nc.scalar.copy(out=b2[:], in_=b2_bank[:, 0:PACK])
        b3_bank = psum.tile([P, PIXELS], BF16, tag="bank")
        for jh in range(J_HALVES):
            cols = slice(jh * BANK, (jh + 1) * BANK)
            nc.tensor.matmul(b3_bank[:, cols], lhsT=ones[:], rhs=b3_row[:, cols], start=True, stop=True)
        b3_all = keep.tile([P, PIXELS], BF16)
        nc.scalar.copy(out=b3_all[:], in_=b3_bank[:])
        a_codes = keep.tile([P, BATCH], U32, align_bytes=64)
        a_scales = keep.tile([P, BATCH], U8, align_bytes=64)
        quantise(nc, a_grouped[:], a_codes[:], a_scales[:])
        w2_codes = keep.tile([P, HIDDEN], U32, align_bytes=64)
        w2_scales = keep.tile([P, HIDDEN], U8, align_bytes=64)
        quantise(nc, w2_grouped[:, w2_quarters[0], :], w2_codes[:, w2_quarters[0]], w2_scales[:, w2_quarters[0]])
        regroup(nc.vector.tensor_copy, w2_grouped[:, w2_quarters[1], :], w2_rows[:, :, w2_quarters[1]])
        quantise(nc, w2_grouped[:, w2_quarters[1], :], w2_codes[:, w2_quarters[1]], w2_scales[:, w2_quarters[1]])
        w3_grouped = []
        for jh in range(J_HALVES):
            grouped = keep.tile([P, BANK, PACK], BF16, align_bytes=64, name="w3_grouped%d" % jh)
            w3_grouped.append(grouped)
        quantise(nc, w2_grouped[:, w2_halves[1], :], w2_codes[:, w2_halves[1]], w2_scales[:, w2_halves[1]])

        z_banks = []
        for t in range(PACK):
            z_bank = psum.tile([P, BATCH], F32, tag="bank")
            h_cols = slice(t * P, (t + 1) * P)
            nc.tensor.matmul_mx(
                out=z_bank[:],
                lhsT=w2_codes[:, h_cols].bitcast(FP8X4),
                lhsT_scale=w2_scales[:, h_cols],
                rhs=a_codes[:].bitcast(FP8X4),
                rhs_scale=a_scales[:],
                start=True,
                stop=True,
            )
            z_banks.append(z_bank)

        w3_codes = keep.tile([P, J_HALVES, BANK], U32, align_bytes=64)
        w3_scales = keep.tile([P, J_HALVES, BANK], U8, align_bytes=64)
        vector_part = slice(0, BANK * 3 // 8)
        scalar_part = slice(BANK * 3 // 8, BANK)
        regroup(nc.vector.tensor_copy, w3_grouped[0][:], w3_rows[0][:])

        exp_y = keep.tile([P, PACK, BATCH], F32)
        relu_y = keep.tile([P, PACK, BATCH], F32)
        last_t = PACK - 1
        nc.vector.tensor_scalar(
            out=relu_y[:, last_t, :], in0=z_banks[last_t][:], scalar1=b2[:, last_t:PACK], scalar2=0.0, op0=ALU.add, op1=ALU.max
        )
        regroup(nc.vector.tensor_copy, w3_grouped[1][:, vector_part, :], w3_rows[1][:, :, vector_part])
        quantise(nc, w3_grouped[0][:], w3_codes[:, 0, :], w3_scales[:, 0, :])
        for t in range(PACK):
            nc.scalar.activation(out=exp_y[:, t, :], in_=z_banks[t][:], func=ACT.Exp, bias=b2[:, t : t + 1], scale=1.0)
            if t < last_t:
                nc.scalar.activation(out=relu_y[:, t, :], in_=z_banks[t][:], func=ACT.Relu, bias=b2[:, t : t + 1], scale=1.0)
        regroup(nc.scalar.copy, w3_grouped[1][:, scalar_part, :], w3_rows[1][:, :, scalar_part])
        nc.scalar.activation(out=warm[:], in_=warm[:], func=ACT.Sigmoid)
        d2_grouped = keep.tile([P, BATCH, PACK], BF16, align_bytes=64)
        for b_cols in b_tiles:
            nc.vector.scalar_tensor_tensor(
                out=d2_grouped[:, b_cols, :],
                in0=exp_y[:, :, b_cols].rearrange("p t b -> p b t"),
                scalar=-1.0,
                in1=relu_y[:, :, b_cols].rearrange("p t b -> p b t"),
                op0=ALU.add,
                op1=ALU.min,
            )
        d2_codes = keep.tile([P, BATCH], U32, align_bytes=64)
        d2_scales = keep.tile([P, BATCH], U8, align_bytes=64)
        for b_cols in b_tiles:
            quantise(nc, d2_grouped[:, b_cols, :], d2_codes[:, b_cols], d2_scales[:, b_cols])
        quantise(nc, w3_grouped[1][:], w3_codes[:, 1, :], w3_scales[:, 1, :])

        v_all = keep.tile([P, B_TILES, PIXELS], F32)
        sig = keep.tile([P, B_TILES, PIXELS], F32)
        pieces = [(0, 0, 0, BANK // 2), (0, 0, BANK // 2, BANK), (0, 1, 0, BANK), (1, 0, 0, BANK), (1, 1, 0, BANK)]
        acc_abs = keep.tile([P, B_TILES, len(pieces) - B_TILES], F32)
        nc.gpsimd.memset(acc_abs[:], 0.0)
        for n, (jh, i, first, last) in enumerate(pieces):
            cols = slice(jh * BANK + first, jh * BANK + last)
            logit_bank = psum.tile([P, last - first], F32, tag="bank")
            nc.tensor.matmul_mx(
                out=logit_bank[:],
                lhsT=d2_codes[:, b_tiles[i]].bitcast(FP8X4),
                lhsT_scale=d2_scales[:, b_tiles[i]],
                rhs=w3_codes[:, jh, first:last].bitcast(FP8X4),
                rhs_scale=w3_scales[:, jh, first:last],
                start=True,
                stop=True,
            )
            nc.vector.tensor_tensor(out=v_all[:, i, cols], in0=logit_bank[:], in1=b3_all[:, cols], op=ALU.add)
            slot = jh if i else jh + (n > 0)
            nc.scalar.activation(
                out=sig[:, i, cols], in_=v_all[:, i, cols], func=ACT.Abs, scale=0.5, accum_out=acc_abs[:, i, slot : slot + 1]
            )
            nc.scalar.activation(out=sig[:, i, cols], in_=sig[:, i, cols], func=ACT.Sigmoid, scale=2.0)
        nc.scalar.activation(out=warm[:], in_=warm[:], func=ACT.Ln)

        acc_xv = keep.tile([P, B_TILES], F32)
        junk = keep.tile([P, PIXELS], F32)
        for i in range(B_TILES):
            nc.vector.scalar_tensor_tensor(
                out=junk[:],
                in0=x_rows[:, i, :],
                scalar=-0.5,
                in1=v_all[:, i, :],
                op0=ALU.add,
                op1=ALU.mult,
                accum_out=acc_xv[:, i : i + 1],
            )
        products = keep.tile([P, B_TILES, PIXELS // FACTORS], F32)
        acc_ln = keep.tile([P, B_TILES], F32)
        sum_abs = keep.tile([P, B_TILES], F32)
        partial = keep.tile([P, B_TILES], F32)
        for i in range(B_TILES):
            nc.vector.tensor_reduce(
                out=products[:, i, :],
                in_=sig[:, i, :].rearrange("p (g f) -> p g f", f=FACTORS),
                axis=AXIS.X,
                op=ALU.mult,
            )
            nc.scalar.activation(out=products[:, i, :], in_=products[:, i, :], func=ACT.Ln, accum_out=acc_ln[:, i : i + 1])
            if i == 0:
                nc.vector.tensor_reduce(out=sum_abs[:], in_=acc_abs[:], axis=AXIS.X, op=ALU.add)
        nc.vector.tensor_tensor(out=partial[:], in0=acc_xv[:], in1=sum_abs[:], op=ALU.subtract)

        nc.vector.tensor_tensor(out=res_pad[:, 0:B_TILES], in0=partial[:], in1=acc_ln[:], op=ALU.add)
        res_rows = keep.tile([P, BLOCK], F32, align_bytes=64)
        nc.vector.transpose(res_rows[:], res_pad[:])
        out_rows = out.rearrange("(i q c) -> i q c", i=B_TILES, c=BLOCK)
        for i, queue in enumerate((nc.sync, nc.scalar)):
            queue.dma_start(out=out_rows[i], in_=res_rows[i : P : BLOCK, :])
